import numpy as np
import ml_dtypes


def mxq(x, axis, fmt="e4m3"):
    dtype, down = {"e4m3": (ml_dtypes.float8_e4m3fn, 7), "e5m2": (ml_dtypes.float8_e5m2, 14)}[fmt]
    v = np.moveaxis(np.asarray(x, np.float32).astype(ml_dtypes.bfloat16).astype(np.float64), axis, -1)
    blocks = v.reshape(v.shape[:-1] + (-1, 32))
    amax = np.abs(blocks).max(-1, keepdims=True)
    byte = np.maximum(np.where(amax > 0, np.frexp(amax)[1] - 1 + 127, 0) - down, 1)
    scale = np.exp2(byte - 127.0)
    codes = (blocks / scale).astype(np.float32).astype(dtype).astype(np.float64)
    return np.moveaxis((codes * scale).reshape(v.shape), -1, axis)


WIDE = False


def mx_kscale(k):
    if not WIDE:
        return np.ones(k)
    levels = np.array([10, -10, 5, -5, 0])
    a = np.random.permutation(np.resize(levels, k // 512 * 4)).reshape(k // 512, 4)
    idx = np.arange(k)
    return np.exp2(a[idx // 512, idx % 128 // 32])


BF16 = ml_dtypes.bfloat16


def bf(x):
    return np.asarray(x, np.float32).astype(BF16)


def f64(x):
    return np.asarray(x).astype(np.float64)


B, N, D = 16, 512, 512
P = 0.125
C = np.sqrt(4.0 / (3.0 * P * N))


def erf(v):
    w = v * v
    acc = np.zeros_like(w)
    for n in range(13):
        c = (n + 0.5) ** 2 / 4.0
        acc += np.exp(-c) / (w + c)
    return np.tanh(2.0 * np.pi * v) - v * np.exp(-w) / np.pi * acc


def gelu(v):
    return 0.5 * v * (1.0 + erf(v / np.sqrt(2.0)))


def draw_adj():
    a = np.random.random((B, N, N)) * (np.random.random((B, N, N)) < P)
    return a * (np.random.random((B, N, 1)) > 0.05)


def setup_inputs():
    s = mx_kscale(N)
    return {"h1": bf(np.random.standard_normal((B, N, D)) * 0.7 / C / s[:, None] * s.mean()),
            "mask": bf(np.random.random((B, N)) > 0.2),
            "adj": bf(draw_adj() * s),
            "W2": bf(np.random.standard_normal((D, D)) * 2.0 / np.sqrt(D)),
            "b2": bf(np.random.standard_normal(D) * 0.3)}


def reference(h1, mask, adj, W2, b2):
    a = f64(adj)
    deg = a.sum(-1)
    dinv = np.where(deg != 0, 1.0 / np.where(deg != 0, deg, 1.0), 0.0)
    adj_n = a * dinv[..., None]
    z = mxq(adj_n, 2, "e4m3") @ mxq(f64(h1), 1, "e4m3")
    g = gelu(z * f64(mask)[..., None])
    return (mxq(g, 2, "e4m3") @ mxq(f64(W2), 1, "e4m3").T) + f64(b2)

@@ -1,0 +1,206 @@
+from contextlib import ExitStack
+
+import concourse.mybir as mybir
+from concourse.masks import make_identity
+
+F32 = mybir.dt.float32
+BF16 = mybir.dt.bfloat16
+U32 = mybir.dt.uint32
+U8 = mybir.dt.uint8
+FP8X4 = mybir.dt.float8_e4m3fn_x4
+ALU = mybir.AluOpType
+ACT = mybir.ActivationFunctionType
+
+B, N, D = 16, 512, 512
+P = 128
+PACK = 4
+TILES = N // P
+HALVES = 2
+
+FLOPS = 2 * B * N * N * D + 2 * B * N * D * D
+
+LOADS_AHEAD = 3
+
+
+def tile_graphconvlayer_pb_t_kernel(tc, h1, mask, adj, W2, b2, out):
+    nc = tc.nc
+    with ExitStack() as ctx:
+        consts = ctx.enter_context(tc.tile_pool(name="consts", bufs=1))
+        work = ctx.enter_context(tc.tile_pool(name="work", bufs=2))
+        psum_t = ctx.enter_context(tc.psum_pool(name="psum_t", bufs=2))
+        psum_mx = ctx.enter_context(tc.psum_pool(name="psum_mx", bufs=6))
+        ctx.enter_context(tc.manual_schedule())
+
+        adj_rows, h1_rows, degs, row_scales = {}, {}, {}, {}
+        adj_mx, h1_groups, h1_mx, g_groups, adj_groups = {}, {}, {}, {}, {}
+
+        def load_graph(g):
+            a_rows = work.tile([P, TILES, N], BF16, bufs=LOADS_AHEAD + 2)
+            nc.sync.dma_start(out=a_rows[:], in_=adj[g].rearrange("(p t) m -> p t m", t=TILES))
+            adj_rows[g] = a_rows
+            h_rows = work.tile([P, PACK, D], BF16, bufs=LOADS_AHEAD + 1)
+            nc.sync.dma_start(
+                out=h_rows[:].rearrange("p (u e) d -> p u e d", u=HALVES),
+                in_=h1[g].rearrange("(u p e) d -> p u e d", u=HALVES, e=2),
+            )
+            h1_rows[g] = h_rows
+
+        load_graph(0)
+        w2_rows = consts.tile([P, TILES, D], BF16)
+        nc.sync.dma_start(out=w2_rows[:], in_=W2.rearrange("(c r) d -> r c d", r=P))
+        for g in range(1, LOADS_AHEAD):
+            load_graph(g)
+
+        mask_cols = consts.tile([P, B, TILES], BF16)
+        bias_rows = consts.tile([P, D], BF16)
+        with nc.allow_non_contiguous_dma(reason="two small loads, once"):
+            nc.scalar.dma_start(out=mask_cols[:], in_=mask.rearrange("b (p t) -> p b t", t=TILES))
+            nc.scalar.dma_start(out=bias_rows[:], in_=b2.partition_broadcast(P))
+
+        ident_f32 = consts.tile([P, P], F32)
+        make_identity(nc, ident_f32[:])
+        ident_bf16 = consts.tile([P, P], BF16)
+        make_identity(nc, ident_bf16[:])
+
+        w2_group = consts.tile([P, D, PACK], BF16, align_bytes=64)
+        for c in range(TILES):
+            w2_t = psum_t.tile([P, PACK, P], BF16, tag="transposed")
+            for j in range(PACK):
+                nc.tensor.transpose(w2_t[:, j, :], w2_rows[:, c, j * P : (j + 1) * P], ident_bf16[:])
+            nc.vector.tensor_copy(
+                out=w2_group[:, c * P : (c + 1) * P, :], in_=w2_t[:].rearrange("p j o -> p o j")
+            )
+        w2_codes = consts.tile([P, D], U32, align_bytes=64)
+        w2_scales = consts.tile([P, D], U8, align_bytes=64)
+        nc.vector.quantize_mx(
+            out=w2_codes[:].bitcast(FP8X4),
+            scales=w2_scales[:],
+            in_=w2_group[:].rearrange("p o j -> p (o j)"),
+        )
+
+        def quantise(group, operand, depth):
+            codes = work.tile([P, N], U32, align_bytes=64, tag=operand + "_codes", bufs=depth)
+            scales = work.tile([P, N], U8, align_bytes=64, tag=operand + "_scales", bufs=depth)
+            nc.vector.quantize_mx(
+                out=codes[:].bitcast(FP8X4),
+                scales=scales[:],
+                in_=group[:].rearrange("p w j -> p (w j)"),
+            )
+            return codes, scales
+
+        def row_sums(g):
+            deg = work.tile([P, TILES], F32)
+            unused = work.tile([P, TILES, N], BF16)
+            for t in range(TILES):
+                nc.scalar.activation(
+                    out=unused[:, t, :], in_=adj_rows[g][:, t, :], func=ACT.Copy,
+                    accum_out=deg[:, t : t + 1],
+                )
+            degs[g] = deg
+
+        def row_factors(g):
+            deg = degs[g]
+            safe = work.tile([P, TILES], F32)
+            nc.vector.scalar_tensor_tensor(
+                out=safe[:], in0=deg[:], scalar=0.0, in1=deg[:], op0=ALU.is_equal, op1=ALU.add
+            )
+            keep = work.tile([P, TILES], F32)
+            nc.vector.scalar_tensor_tensor(
+                out=keep[:], in0=deg[:], scalar=0.0, in1=mask_cols[:, g, :],
+                op0=ALU.not_equal, op1=ALU.mult,
+            )
+            inverse = work.tile([P, TILES], F32)
+            nc.vector.reciprocal(out=inverse[:], in_=safe[:])
+            factor = work.tile([P, TILES], F32)
+            nc.vector.tensor_tensor(out=factor[:], in0=inverse[:], in1=keep[:], op=ALU.mult)
+            row_scales[g] = factor
+
+        def normalise_and_transpose(g):
+            adj_n = work.tile([P, TILES, N], BF16)
+            for t in range(TILES):
+                nc.vector.tensor_scalar(
+                    out=adj_n[:, t, :], in0=adj_rows[g][:, t, :],
+                    scalar1=row_scales[g][:, t : t + 1], scalar2=None, op0=ALU.mult,
+                )
+            adj_words = adj_n[:].bitcast(F32)
+            group = work.tile([P, N, PACK], BF16, align_bytes=64)
+            group_words = group[:].bitcast(F32)
+            for pair in range(TILES // 2):
+                turned = psum_t.tile([P, 2, HALVES, P], F32, tag="transposed")
+                for s in range(2):
+                    for u in range(HALVES):
+                        nc.tensor.transpose(
+                            turned[:, s, u, :],
+                            adj_words[:, 2 * pair + s, u * P : (u + 1) * P],
+                            ident_f32[:],
+                        )
+                nc.scalar.copy(
+                    out=group_words[:, 2 * pair * P : (2 * pair + 2) * P, :].rearrange(
+                        "p (s n) u -> p s n u", s=2
+                    ),
+                    in_=turned[:].rearrange("p s u n -> p s n u"),
+                )
+            adj_groups[g] = group
+
+        def regroup_h1(g):
+            group = work.tile([P, D, PACK], BF16, align_bytes=64)
+            nc.vector.tensor_copy(
+                out=group[:].rearrange("p (c i) j -> p c j i", i=4),
+                in_=h1_rows[g][:].rearrange("p j (c i) -> p c j i", i=4),
+            )
+            h1_groups[g] = group
+
+        def aggregate(g):
+            a_codes, a_scales = adj_mx[g]
+            h_codes, h_scales = h1_mx[g]
+            group = work.tile([P, N, PACK], BF16, align_bytes=64)
+            for c in range(TILES):
+                nodes = slice(c * P, (c + 1) * P)
+                z_t = psum_mx.tile([P, PACK, P], F32, tag="mx")
+                for j in range(PACK):
+                    feats = slice(j * P, (j + 1) * P)
+                    nc.tensor.matmul_mx(
+                        out=z_t[:, j, :],
+                        lhsT=h_codes[:, feats].bitcast(FP8X4), lhsT_scale=h_scales[:, feats],
+                        rhs=a_codes[:, nodes].bitcast(FP8X4), rhs_scale=a_scales[:, nodes],
+                        start=True, stop=True,
+                    )
+                nc.scalar.activation(
+                    out=group[:, nodes, :], in_=z_t[:].rearrange("p j n -> p n j"), func=ACT.Gelu
+                )
+            g_groups[g] = group
+
+        def project(g, g_codes, g_scales):
+            result = work.tile([P, TILES, D], F32, bufs=3)
+            for c in range(TILES):
+                nodes = slice(c * P, (c + 1) * P)
+                acc = psum_mx.tile([P, D], F32, tag="mx")
+                nc.tensor.matmul_mx(
+                    out=acc[:],
+                    lhsT=g_codes[:, nodes].bitcast(FP8X4), lhsT_scale=g_scales[:, nodes],
+                    rhs=w2_codes[:].bitcast(FP8X4), rhs_scale=w2_scales[:],
+                    start=True, stop=True,
+                )
+                nc.vector.tensor_tensor(out=result[:, c, :], in0=acc[:], in1=bias_rows[:], op=ALU.add)
+            nc.sync.dma_start(out=out[g].rearrange("(p t) o -> p t o", t=TILES), in_=result[:])
+
+        for i in range(B + 3):
+            if i + LOADS_AHEAD < B:
+                load_graph(i + LOADS_AHEAD)
+            if i < B:
+                row_sums(i)
+            if 0 <= i - 1 < B:
+                normalise_and_transpose(i - 1)
+            if 0 <= i - 3 < B:
+                g_mx = quantise(g_groups[i - 3], "g", 2)
+            if 0 <= i - 2 < B:
+                adj_mx[i - 2] = quantise(adj_groups[i - 2], "adj", 2)
+            if i < B:
+                regroup_h1(i)
+            if 0 <= i - 3 < B:
+                project(i - 3, g_mx[0], g_mx[1])
+            if 0 <= i - 2 < B:
+                aggregate(i - 2)
+            if i < B:
+                h1_mx[i] = quantise(h1_groups[i], "h1", 3)
+                row_factors(i)

@@ -19,6 +19,7 @@ HALVES = 2
 
 FLOPS = 2 * B * N * N * D + 2 * B * N * D * D
 
+W2_ROUND = 2
 LOADS_AHEAD = 3
 
 
@@ -46,10 +47,10 @@ def tile_graphconvlayer_pb_t_kernel(tc, h1, mask, adj, W2, b2, out):
             h1_rows[g] = h_rows
 
         load_graph(0)
+        load_graph(1)
         w2_rows = consts.tile([P, TILES, D], BF16)
         nc.sync.dma_start(out=w2_rows[:], in_=W2.rearrange("(c r) d -> r c d", r=P))
-        for g in range(1, LOADS_AHEAD):
-            load_graph(g)
+        load_graph(2)
 
         mask_cols = consts.tile([P, B, TILES], BF16)
         bias_rows = consts.tile([P, D], BF16)
@@ -62,21 +63,28 @@ def tile_graphconvlayer_pb_t_kernel(tc, h1, mask, adj, W2, b2, out):
         ident_bf16 = consts.tile([P, P], BF16)
         make_identity(nc, ident_bf16[:])
 
+        table_warmer = consts.tile([P, 1], F32)
+        nc.scalar.activation(out=table_warmer[:], in_=ident_f32[:, 0:1], func=ACT.Gelu)
+
         w2_group = consts.tile([P, D, PACK], BF16, align_bytes=64)
-        for c in range(TILES):
-            w2_t = psum_t.tile([P, PACK, P], BF16, tag="transposed")
-            for j in range(PACK):
-                nc.tensor.transpose(w2_t[:, j, :], w2_rows[:, c, j * P : (j + 1) * P], ident_bf16[:])
-            nc.vector.tensor_copy(
-                out=w2_group[:, c * P : (c + 1) * P, :], in_=w2_t[:].rearrange("p j o -> p o j")
-            )
         w2_codes = consts.tile([P, D], U32, align_bytes=64)
         w2_scales = consts.tile([P, D], U8, align_bytes=64)
-        nc.vector.quantize_mx(
-            out=w2_codes[:].bitcast(FP8X4),
-            scales=w2_scales[:],
-            in_=w2_group[:].rearrange("p o j -> p (o j)"),
-        )
+
+        def prepare_w2():
+            for c in range(TILES):
+                w2_t = psum_t.tile([P, PACK, P], BF16, tag="transposed")
+                for j in range(PACK):
+                    nc.tensor.transpose(
+                        w2_t[:, j, :], w2_rows[:, c, j * P : (j + 1) * P], ident_bf16[:]
+                    )
+                nc.vector.tensor_copy(
+                    out=w2_group[:, c * P : (c + 1) * P, :], in_=w2_t[:].rearrange("p j o -> p o j")
+                )
+            nc.vector.quantize_mx(
+                out=w2_codes[:].bitcast(FP8X4),
+                scales=w2_scales[:],
+                in_=w2_group[:].rearrange("p o j -> p (o j)"),
+            )
 
         def quantise(group, operand, depth):
             codes = work.tile([P, N], U32, align_bytes=64, tag=operand + "_codes", bufs=depth)
@@ -123,8 +131,8 @@ def tile_graphconvlayer_pb_t_kernel(tc, h1, mask, adj, W2, b2, out):
                     scalar1=row_scales[g][:, t : t + 1], scalar2=None, op0=ALU.mult,
                 )
             adj_words = adj_n[:].bitcast(F32)
-            group = work.tile([P, N, PACK], BF16, align_bytes=64)
-            group_words = group[:].bitcast(F32)
+            adj_group = work.tile([P, N, PACK], BF16, align_bytes=64)
+            group_words = adj_group[:].bitcast(F32)
             for pair in range(TILES // 2):
                 turned = psum_t.tile([P, 2, HALVES, P], F32, tag="transposed")
                 for s in range(2):
@@ -140,20 +148,20 @@ def tile_graphconvlayer_pb_t_kernel(tc, h1, mask, adj, W2, b2, out):
                     ),
                     in_=turned[:].rearrange("p s u n -> p s n u"),
                 )
-            adj_groups[g] = group
+            adj_groups[g] = adj_group
 
         def regroup_h1(g):
-            group = work.tile([P, D, PACK], BF16, align_bytes=64)
+            h1_group = work.tile([P, D, PACK], BF16, align_bytes=64)
             nc.vector.tensor_copy(
-                out=group[:].rearrange("p (c i) j -> p c j i", i=4),
+                out=h1_group[:].rearrange("p (c i) j -> p c j i", i=4),
                 in_=h1_rows[g][:].rearrange("p j (c i) -> p c j i", i=4),
             )
-            h1_groups[g] = group
+            h1_groups[g] = h1_group
 
         def aggregate(g):
             a_codes, a_scales = adj_mx[g]
             h_codes, h_scales = h1_mx[g]
-            group = work.tile([P, N, PACK], BF16, align_bytes=64)
+            g_group = work.tile([P, N, PACK], BF16, align_bytes=64)
             for c in range(TILES):
                 nodes = slice(c * P, (c + 1) * P)
                 z_t = psum_mx.tile([P, PACK, P], F32, tag="mx")
@@ -166,12 +174,13 @@ def tile_graphconvlayer_pb_t_kernel(tc, h1, mask, adj, W2, b2, out):
                         start=True, stop=True,
                     )
                 nc.scalar.activation(
-                    out=group[:, nodes, :], in_=z_t[:].rearrange("p j n -> p n j"), func=ACT.Gelu
+                    out=g_group[:, nodes, :], in_=z_t[:].rearrange("p j n -> p n j"), func=ACT.Gelu
                 )
-            g_groups[g] = group
+            g_groups[g] = g_group
 
         def project(g, g_codes, g_scales):
             result = work.tile([P, TILES, D], F32, bufs=3)
+            out_rows = out[g].rearrange("(p t) o -> p t o", t=TILES)
             for c in range(TILES):
                 nodes = slice(c * P, (c + 1) * P)
                 acc = psum_mx.tile([P, D], F32, tag="mx")
@@ -182,7 +191,7 @@ def tile_graphconvlayer_pb_t_kernel(tc, h1, mask, adj, W2, b2, out):
                     start=True, stop=True,
                 )
                 nc.vector.tensor_tensor(out=result[:, c, :], in0=acc[:], in1=bias_rows[:], op=ALU.add)
-            nc.sync.dma_start(out=out[g].rearrange("(p t) o -> p t o", t=TILES), in_=result[:])
+                nc.sync.dma_start(out=out_rows[:, c, :], in_=result[:, c, :])
 
         for i in range(B + 3):
             if i + LOADS_AHEAD < B:
@@ -204,3 +213,5 @@ def tile_graphconvlayer_pb_t_kernel(tc, h1, mask, adj, W2, b2, out):
             if i < B:
                 h1_mx[i] = quantise(h1_groups[i], "h1", 3)
                 row_factors(i)
+            if i == W2_ROUND:
+                prepare_w2()

@@ -151,11 +151,14 @@ def tile_graphconvlayer_pb_t_kernel(tc, h1, mask, adj, W2, b2, out):
             adj_groups[g] = adj_group
 
         def regroup_h1(g):
-            h1_group = work.tile([P, D, PACK], BF16, align_bytes=64)
-            nc.vector.tensor_copy(
-                out=h1_group[:].rearrange("p (c i) j -> p c j i", i=4),
-                in_=h1_rows[g][:].rearrange("p j (c i) -> p c j i", i=4),
-            )
+            h1_group = work.tile([P, D, PACK], BF16, align_bytes=64, bufs=3)
+            for c in range(TILES):
+                feats = slice(c * P, (c + 1) * P)
+                nc.gpsimd.tensor_scalar(
+                    out=h1_group[:, feats, :],
+                    in0=h1_rows[g][:, :, feats].rearrange("p j d -> p d j"),
+                    scalar1=1.0, scalar2=0.0, op0=ALU.mult, op1=ALU.add,
+                )
             h1_groups[g] = h1_group
 
         def aggregate(g):
@@ -193,6 +196,7 @@ def tile_graphconvlayer_pb_t_kernel(tc, h1, mask, adj, W2, b2, out):
                 nc.vector.tensor_tensor(out=result[:, c, :], in0=acc[:], in1=bias_rows[:], op=ALU.add)
                 nc.sync.dma_start(out=out_rows[:, c, :], in_=result[:, c, :])
 
+        regroup_h1(0)
         for i in range(B + 3):
             if i + LOADS_AHEAD < B:
                 load_graph(i + LOADS_AHEAD)
@@ -204,8 +208,8 @@ def tile_graphconvlayer_pb_t_kernel(tc, h1, mask, adj, W2, b2, out):
                 g_mx = quantise(g_groups[i - 3], "g", 2)
             if 0 <= i - 2 < B:
                 adj_mx[i - 2] = quantise(adj_groups[i - 2], "adj", 2)
-            if i < B:
-                regroup_h1(i)
+            if i + 1 < B:
+                regroup_h1(i + 1)
             if 0 <= i - 3 < B:
                 project(i - 3, g_mx[0], g_mx[1])
             if 0 <= i - 2 < B:

@@ -32,7 +32,7 @@ def tile_graphconvlayer_pb_t_kernel(tc, h1, mask, adj, W2, b2, out):
         psum_mx = ctx.enter_context(tc.psum_pool(name="psum_mx", bufs=6))
         ctx.enter_context(tc.manual_schedule())
 
-        adj_rows, h1_rows, degs, row_scales = {}, {}, {}, {}
+        adj_rows, h1_rows, degs, safes, keeps, inverses = {}, {}, {}, {}, {}, {}
         adj_mx, h1_groups, h1_mx, g_groups, adj_groups = {}, {}, {}, {}, {}
 
         def load_graph(g):
@@ -106,7 +106,7 @@ def tile_graphconvlayer_pb_t_kernel(tc, h1, mask, adj, W2, b2, out):
                 )
             degs[g] = deg
 
-        def row_factors(g):
+        def row_guards(g):
             deg = degs[g]
             safe = work.tile([P, TILES], F32)
             nc.vector.scalar_tensor_tensor(
@@ -117,18 +117,20 @@ def tile_graphconvlayer_pb_t_kernel(tc, h1, mask, adj, W2, b2, out):
                 out=keep[:], in0=deg[:], scalar=0.0, in1=mask_cols[:, g, :],
                 op0=ALU.not_equal, op1=ALU.mult,
             )
+            safes[g], keeps[g] = safe, keep
+
+        def row_inverses(g):
             inverse = work.tile([P, TILES], F32)
-            nc.vector.reciprocal(out=inverse[:], in_=safe[:])
-            factor = work.tile([P, TILES], F32)
-            nc.vector.tensor_tensor(out=factor[:], in0=inverse[:], in1=keep[:], op=ALU.mult)
-            row_scales[g] = factor
+            nc.vector.reciprocal(out=inverse[:], in_=safes[g][:])
+            inverses[g] = inverse
 
         def normalise_and_transpose(g):
             adj_n = work.tile([P, TILES, N], BF16)
             for t in range(TILES):
                 nc.vector.tensor_scalar(
                     out=adj_n[:, t, :], in0=adj_rows[g][:, t, :],
-                    scalar1=row_scales[g][:, t : t + 1], scalar2=None, op0=ALU.mult,
+                    scalar1=inverses[g][:, t : t + 1], scalar2=keeps[g][:, t : t + 1],
+                    op0=ALU.mult, op1=ALU.mult,
                 )
             adj_words = adj_n[:].bitcast(F32)
             adj_group = work.tile([P, N, PACK], BF16, align_bytes=64)
@@ -151,14 +153,11 @@ def tile_graphconvlayer_pb_t_kernel(tc, h1, mask, adj, W2, b2, out):
             adj_groups[g] = adj_group
 
         def regroup_h1(g):
-            h1_group = work.tile([P, D, PACK], BF16, align_bytes=64, bufs=3)
-            for c in range(TILES):
-                feats = slice(c * P, (c + 1) * P)
-                nc.gpsimd.tensor_scalar(
-                    out=h1_group[:, feats, :],
-                    in0=h1_rows[g][:, :, feats].rearrange("p j d -> p d j"),
-                    scalar1=1.0, scalar2=0.0, op0=ALU.mult, op1=ALU.add,
-                )
+            h1_group = work.tile([P, D, PACK], BF16, align_bytes=64)
+            nc.vector.tensor_copy(
+                out=h1_group[:].rearrange("p (c i) j -> p c j i", i=4),
+                in_=h1_rows[g][:].rearrange("p j (c i) -> p c j i", i=4),
+            )
             h1_groups[g] = h1_group
 
         def aggregate(g):
@@ -196,7 +195,6 @@ def tile_graphconvlayer_pb_t_kernel(tc, h1, mask, adj, W2, b2, out):
                 nc.vector.tensor_tensor(out=result[:, c, :], in0=acc[:], in1=bias_rows[:], op=ALU.add)
                 nc.sync.dma_start(out=out_rows[:, c, :], in_=result[:, c, :])
 
-        regroup_h1(0)
         for i in range(B + 3):
             if i + LOADS_AHEAD < B:
                 load_graph(i + LOADS_AHEAD)
@@ -208,14 +206,16 @@ def tile_graphconvlayer_pb_t_kernel(tc, h1, mask, adj, W2, b2, out):
                 g_mx = quantise(g_groups[i - 3], "g", 2)
             if 0 <= i - 2 < B:
                 adj_mx[i - 2] = quantise(adj_groups[i - 2], "adj", 2)
-            if i + 1 < B:
-                regroup_h1(i + 1)
+            if i < B:
+                regroup_h1(i)
+                row_guards(i)
             if 0 <= i - 3 < B:
                 project(i - 3, g_mx[0], g_mx[1])
+            if i < B:
+                row_inverses(i)
             if 0 <= i - 2 < B:
                 aggregate(i - 2)
             if i < B:
                 h1_mx[i] = quantise(h1_groups[i], "h1", 3)
-                row_factors(i)
             if i == W2_ROUND:
                 prepare_w2()

@@ -30,7 +30,6 @@ def tile_graphconvlayer_pb_t_kernel(tc, h1, mask, adj, W2, b2, out):
         work = ctx.enter_context(tc.tile_pool(name="work", bufs=2))
         psum_t = ctx.enter_context(tc.psum_pool(name="psum_t", bufs=2))
         psum_mx = ctx.enter_context(tc.psum_pool(name="psum_mx", bufs=6))
-        ctx.enter_context(tc.manual_schedule())
 
         adj_rows, h1_rows, degs, safes, keeps, inverses = {}, {}, {}, {}, {}, {}
         adj_mx, h1_groups, h1_mx, g_groups, adj_groups = {}, {}, {}, {}, {}

@@ -20,6 +20,7 @@ HALVES = 2
 FLOPS = 2 * B * N * N * D + 2 * B * N * D * D
 
 W2_ROUND = 2
+G_PIECES = 2
 LOADS_AHEAD = 3
 
 
@@ -30,6 +31,7 @@ def tile_graphconvlayer_pb_t_kernel(tc, h1, mask, adj, W2, b2, out):
         work = ctx.enter_context(tc.tile_pool(name="work", bufs=2))
         psum_t = ctx.enter_context(tc.psum_pool(name="psum_t", bufs=2))
         psum_mx = ctx.enter_context(tc.psum_pool(name="psum_mx", bufs=6))
+        ctx.enter_context(tc.manual_schedule())
 
         adj_rows, h1_rows, degs, safes, keeps, inverses = {}, {}, {}, {}, {}, {}
         adj_mx, h1_groups, h1_mx, g_groups, adj_groups = {}, {}, {}, {}, {}
@@ -85,14 +87,17 @@ def tile_graphconvlayer_pb_t_kernel(tc, h1, mask, adj, W2, b2, out):
                 in_=w2_group[:].rearrange("p o j -> p (o j)"),
             )
 
-        def quantise(group, operand, depth):
+        def quantise(group, operand, depth, pieces):
             codes = work.tile([P, N], U32, align_bytes=64, tag=operand + "_codes", bufs=depth)
             scales = work.tile([P, N], U8, align_bytes=64, tag=operand + "_scales", bufs=depth)
-            nc.vector.quantize_mx(
-                out=codes[:].bitcast(FP8X4),
-                scales=scales[:],
-                in_=group[:].rearrange("p w j -> p (w j)"),
-            )
+            width = N // pieces
+            for k in range(pieces):
+                cols = slice(k * width, (k + 1) * width)
+                nc.vector.quantize_mx(
+                    out=codes[:, cols].bitcast(FP8X4),
+                    scales=scales[:, cols],
+                    in_=group[:, cols, :].rearrange("p w j -> p (w j)"),
+                )
             return codes, scales
 
         def row_sums(g):
@@ -202,9 +207,9 @@ def tile_graphconvlayer_pb_t_kernel(tc, h1, mask, adj, W2, b2, out):
             if 0 <= i - 1 < B:
                 normalise_and_transpose(i - 1)
             if 0 <= i - 3 < B:
-                g_mx = quantise(g_groups[i - 3], "g", 2)
+                g_mx = quantise(g_groups[i - 3], "g", 2, G_PIECES)
             if 0 <= i - 2 < B:
-                adj_mx[i - 2] = quantise(adj_groups[i - 2], "adj", 2)
+                adj_mx[i - 2] = quantise(adj_groups[i - 2], "adj", 2, 1)
             if i < B:
                 regroup_h1(i)
                 row_guards(i)
@@ -215,6 +220,6 @@ def tile_graphconvlayer_pb_t_kernel(tc, h1, mask, adj, W2, b2, out):
             if 0 <= i - 2 < B:
                 aggregate(i - 2)
             if i < B:
-                h1_mx[i] = quantise(h1_groups[i], "h1", 3)
+                h1_mx[i] = quantise(h1_groups[i], "h1", 3, 1)
             if i == W2_ROUND:
                 prepare_w2()

@@ -21,6 +21,9 @@ FLOPS = 2 * B * N * N * D + 2 * B * N * D * D
 
 W2_ROUND = 2
 G_PIECES = 2
+FOLD = 32
+SCALAR_SUMS = 5
+H1_SCALAR_COLS = 384
 LOADS_AHEAD = 3
 
 
@@ -30,11 +33,13 @@ def tile_graphconvlayer_pb_t_kernel(tc, h1, mask, adj, W2, b2, out):
         consts = ctx.enter_context(tc.tile_pool(name="consts", bufs=1))
         work = ctx.enter_context(tc.tile_pool(name="work", bufs=2))
         psum_t = ctx.enter_context(tc.psum_pool(name="psum_t", bufs=2))
-        psum_mx = ctx.enter_context(tc.psum_pool(name="psum_mx", bufs=6))
+        psum_f = ctx.enter_context(tc.psum_pool(name="psum_f", bufs=1))
+        psum_mx = ctx.enter_context(tc.psum_pool(name="psum_mx", bufs=5))
         ctx.enter_context(tc.manual_schedule())
 
         adj_rows, h1_rows, degs, safes, keeps, inverses = {}, {}, {}, {}, {}, {}
         adj_mx, h1_groups, h1_mx, g_groups, adj_groups = {}, {}, {}, {}, {}
+        folds = {}
 
         def load_graph(g):
             a_rows = work.tile([P, TILES, N], BF16, bufs=LOADS_AHEAD + 2)
@@ -102,16 +107,30 @@ def tile_graphconvlayer_pb_t_kernel(tc, h1, mask, adj, W2, b2, out):
 
         def row_sums(g):
             deg = work.tile([P, TILES], F32)
+            degs[g] = deg
+            if g % SCALAR_SUMS != 0:
+                folded = psum_f.tile([P, TILES, FOLD], F32)
+                for k in range(N // FOLD):
+                    nc.tensor.matmul(
+                        folded[:], lhsT=ident_bf16[:],
+                        rhs=adj_rows[g][:, :, k * FOLD : (k + 1) * FOLD],
+                        start=(k == 0), stop=(k == N // FOLD - 1),
+                    )
+                folds[g] = folded
+                return
             unused = work.tile([P, TILES, N], BF16)
             for t in range(TILES):
                 nc.scalar.activation(
                     out=unused[:, t, :], in_=adj_rows[g][:, t, :], func=ACT.Copy,
                     accum_out=deg[:, t : t + 1],
                 )
-            degs[g] = deg
 
         def row_guards(g):
             deg = degs[g]
+            if g in folds:
+                nc.vector.tensor_reduce(
+                    out=deg[:], in_=folds[g][:], axis=mybir.AxisListType.X, op=ALU.add
+                )
             safe = work.tile([P, TILES], F32)
             nc.vector.scalar_tensor_tensor(
                 out=safe[:], in0=deg[:], scalar=0.0, in1=deg[:], op0=ALU.is_equal, op1=ALU.add
@@ -156,13 +175,14 @@ def tile_graphconvlayer_pb_t_kernel(tc, h1, mask, adj, W2, b2, out):
                 )
             adj_groups[g] = adj_group
 
-        def regroup_h1(g):
-            h1_group = work.tile([P, D, PACK], BF16, align_bytes=64)
-            nc.vector.tensor_copy(
-                out=h1_group[:].rearrange("p (c i) j -> p c j i", i=4),
-                in_=h1_rows[g][:].rearrange("p j (c i) -> p c j i", i=4),
+        def regroup_h1(g, copy, cols):
+            if g not in h1_groups:
+                h1_group = work.tile([P, D, PACK], BF16, align_bytes=64)
+                h1_groups[g] = h1_group
+            copy(
+                out=h1_groups[g][:, cols, :].rearrange("p (c i) j -> p c j i", i=4),
+                in_=h1_rows[g][:, :, cols].rearrange("p j (c i) -> p c j i", i=4),
             )
-            h1_groups[g] = h1_group
 
         def aggregate(g):
             a_codes, a_scales = adj_mx[g]
@@ -204,6 +224,9 @@ def tile_graphconvlayer_pb_t_kernel(tc, h1, mask, adj, W2, b2, out):
                 load_graph(i + LOADS_AHEAD)
             if i < B:
                 row_sums(i)
+                scalar_cols = 0 if i % SCALAR_SUMS == 0 else H1_SCALAR_COLS
+                if scalar_cols > 0:
+                    regroup_h1(i, nc.scalar.copy, slice(0, scalar_cols))
             if 0 <= i - 1 < B:
                 normalise_and_transpose(i - 1)
             if 0 <= i - 3 < B:
@@ -211,7 +234,7 @@ def tile_graphconvlayer_pb_t_kernel(tc, h1, mask, adj, W2, b2, out):
             if 0 <= i - 2 < B:
                 adj_mx[i - 2] = quantise(adj_groups[i - 2], "adj", 2, 1)
             if i < B:
-                regroup_h1(i)
+                regroup_h1(i, nc.vector.tensor_copy, slice(scalar_cols, D))
                 row_guards(i)
             if 0 <= i - 3 < B:
                 project(i - 3, g_mx[0], g_mx[1])

@@ -37,7 +37,7 @@ def tile_graphconvlayer_pb_t_kernel(tc, h1, mask, adj, W2, b2, out):
         psum_mx = ctx.enter_context(tc.psum_pool(name="psum_mx", bufs=5))
         ctx.enter_context(tc.manual_schedule())
 
-        adj_rows, h1_rows, degs, safes, keeps, inverses = {}, {}, {}, {}, {}, {}
+        adj_rows, h1_rows, degs, safes, inverses = {}, {}, {}, {}, {}
         adj_mx, h1_groups, h1_mx, g_groups, adj_groups = {}, {}, {}, {}, {}
         folds = {}
 
@@ -58,11 +58,10 @@ def tile_graphconvlayer_pb_t_kernel(tc, h1, mask, adj, W2, b2, out):
         nc.sync.dma_start(out=w2_rows[:], in_=W2.rearrange("(c r) d -> r c d", r=P))
         load_graph(2)
 
-        mask_cols = consts.tile([P, B, TILES], BF16)
-        bias_rows = consts.tile([P, D], BF16)
-        with nc.allow_non_contiguous_dma(reason="two small loads, once"):
-            nc.scalar.dma_start(out=mask_cols[:], in_=mask.rearrange("b (p t) -> p b t", t=TILES))
-            nc.scalar.dma_start(out=bias_rows[:], in_=b2.partition_broadcast(P))
+        small_rows = consts.tile([P, D], BF16)
+        nc.gpsimd.memset(small_rows[:], 0.0)
+        nc.scalar.dma_start(out=small_rows[0:B, :], in_=mask)
+        nc.scalar.dma_start(out=small_rows[B : B + 1, :], in_=b2.unsqueeze(0))
 
         ident_f32 = consts.tile([P, P], F32)
         make_identity(nc, ident_f32[:])
@@ -71,6 +70,23 @@ def tile_graphconvlayer_pb_t_kernel(tc, h1, mask, adj, W2, b2, out):
 
         table_warmer = consts.tile([P, 1], F32)
         nc.scalar.activation(out=table_warmer[:], in_=ident_f32[:, 0:1], func=ACT.Gelu)
+
+        mask_cols = consts.tile([P, TILES, B], F32)
+        bias_rows = consts.tile([P, D], BF16)
+
+        def spread_mask():
+            mask_t = psum_t.tile([P, TILES, P], BF16, tag="transposed")
+            for t in range(TILES):
+                nc.tensor.transpose(mask_t[:, t, :], small_rows[:, t::TILES], ident_bf16[:])
+            nc.scalar.copy(out=mask_cols[:], in_=mask_t[:, :, 0:B])
+
+        def spread_bias():
+            bias_all = psum_mx.tile([P, D], F32, tag="mx")
+            nc.tensor.matmul(
+                bias_all[:], lhsT=ident_bf16[:, B : B + 1].to_broadcast([P, P]), rhs=small_rows[:],
+                start=True, stop=True,
+            )
+            nc.scalar.copy(out=bias_rows[:], in_=bias_all[:])
 
         w2_group = consts.tile([P, D, PACK], BF16, align_bytes=64)
         w2_codes = consts.tile([P, D], U32, align_bytes=64)
@@ -125,22 +141,19 @@ def tile_graphconvlayer_pb_t_kernel(tc, h1, mask, adj, W2, b2, out):
                     accum_out=deg[:, t : t + 1],
                 )
 
-        def row_guards(g):
-            deg = degs[g]
+        def add_folds(g):
             if g in folds:
                 nc.vector.tensor_reduce(
-                    out=deg[:], in_=folds[g][:], axis=mybir.AxisListType.X, op=ALU.add
+                    out=degs[g][:], in_=folds[g][:], axis=mybir.AxisListType.X, op=ALU.add
                 )
+
+        def row_guards(g):
+            deg = degs[g]
             safe = work.tile([P, TILES], F32)
             nc.vector.scalar_tensor_tensor(
                 out=safe[:], in0=deg[:], scalar=0.0, in1=deg[:], op0=ALU.is_equal, op1=ALU.add
             )
-            keep = work.tile([P, TILES], F32)
-            nc.vector.scalar_tensor_tensor(
-                out=keep[:], in0=deg[:], scalar=0.0, in1=mask_cols[:, g, :],
-                op0=ALU.not_equal, op1=ALU.mult,
-            )
-            safes[g], keeps[g] = safe, keep
+            safes[g] = safe
 
         def row_inverses(g):
             inverse = work.tile([P, TILES], F32)
@@ -152,7 +165,7 @@ def tile_graphconvlayer_pb_t_kernel(tc, h1, mask, adj, W2, b2, out):
             for t in range(TILES):
                 nc.vector.tensor_scalar(
                     out=adj_n[:, t, :], in0=adj_rows[g][:, t, :],
-                    scalar1=inverses[g][:, t : t + 1], scalar2=keeps[g][:, t : t + 1],
+                    scalar1=inverses[g][:, t : t + 1], scalar2=mask_cols[:, t, g : g + 1],
                     op0=ALU.mult, op1=ALU.mult,
                 )
             adj_words = adj_n[:].bitcast(F32)
@@ -224,6 +237,9 @@ def tile_graphconvlayer_pb_t_kernel(tc, h1, mask, adj, W2, b2, out):
                 load_graph(i + LOADS_AHEAD)
             if i < B:
                 row_sums(i)
+                if i == 0:
+                    spread_mask()
+                    spread_bias()
                 scalar_cols = 0 if i % SCALAR_SUMS == 0 else H1_SCALAR_COLS
                 if scalar_cols > 0:
                     regroup_h1(i, nc.scalar.copy, slice(0, scalar_cols))
@@ -234,6 +250,7 @@ def tile_graphconvlayer_pb_t_kernel(tc, h1, mask, adj, W2, b2, out):
             if 0 <= i - 2 < B:
                 adj_mx[i - 2] = quantise(adj_groups[i - 2], "adj", 2, 1)
             if i < B:
+                add_folds(i)
                 regroup_h1(i, nc.vector.tensor_copy, slice(scalar_cols, D))
                 row_guards(i)
             if 0 <= i - 3 < B:

@@ -22,8 +22,9 @@ FLOPS = 2 * B * N * N * D + 2 * B * N * D * D
 W2_ROUND = 2
 G_PIECES = 2
 FOLD = 32
-SCALAR_SUMS = 5
+SCALAR_SUMS = (0, 1, 6, 11)
 H1_SCALAR_COLS = 384
+H1_GPSIMD_COLS = 128
 LOADS_AHEAD = 3
 
 
@@ -41,10 +42,12 @@ def tile_graphconvlayer_pb_t_kernel(tc, h1, mask, adj, W2, b2, out):
         adj_mx, h1_groups, h1_mx, g_groups, adj_groups = {}, {}, {}, {}, {}
         folds = {}
 
-        def load_graph(g):
+        def load_adj(g):
             a_rows = work.tile([P, TILES, N], BF16, bufs=LOADS_AHEAD + 2)
             nc.sync.dma_start(out=a_rows[:], in_=adj[g].rearrange("(p t) m -> p t m", t=TILES))
             adj_rows[g] = a_rows
+
+        def load_h1(g):
             h_rows = work.tile([P, PACK, D], BF16, bufs=LOADS_AHEAD + 1)
             nc.sync.dma_start(
                 out=h_rows[:].rearrange("p (u e) d -> p u e d", u=HALVES),
@@ -52,16 +55,21 @@ def tile_graphconvlayer_pb_t_kernel(tc, h1, mask, adj, W2, b2, out):
             )
             h1_rows[g] = h_rows
 
-        load_graph(0)
+        def load_graph(g):
+            load_adj(g)
+            load_h1(g)
+
+        small_rows = consts.tile([P, D], BF16)
+        nc.gpsimd.memset(small_rows[:], 0.0)
+
+        load_adj(0)
+        nc.sync.dma_start(out=small_rows[0:B, :], in_=mask)
+        nc.sync.dma_start(out=small_rows[B : B + 1, :], in_=b2.unsqueeze(0))
+        load_h1(0)
         load_graph(1)
         w2_rows = consts.tile([P, TILES, D], BF16)
         nc.sync.dma_start(out=w2_rows[:], in_=W2.rearrange("(c r) d -> r c d", r=P))
         load_graph(2)
-
-        small_rows = consts.tile([P, D], BF16)
-        nc.gpsimd.memset(small_rows[:], 0.0)
-        nc.scalar.dma_start(out=small_rows[0:B, :], in_=mask)
-        nc.scalar.dma_start(out=small_rows[B : B + 1, :], in_=b2.unsqueeze(0))
 
         ident_f32 = consts.tile([P, P], F32)
         make_identity(nc, ident_f32[:])
@@ -92,16 +100,18 @@ def tile_graphconvlayer_pb_t_kernel(tc, h1, mask, adj, W2, b2, out):
         w2_codes = consts.tile([P, D], U32, align_bytes=64)
         w2_scales = consts.tile([P, D], U8, align_bytes=64)
 
-        def prepare_w2():
+        def transpose_w2():
             for c in range(TILES):
                 w2_t = psum_t.tile([P, PACK, P], BF16, tag="transposed")
                 for j in range(PACK):
                     nc.tensor.transpose(
                         w2_t[:, j, :], w2_rows[:, c, j * P : (j + 1) * P], ident_bf16[:]
                     )
-                nc.vector.tensor_copy(
+                nc.scalar.copy(
                     out=w2_group[:, c * P : (c + 1) * P, :], in_=w2_t[:].rearrange("p j o -> p o j")
                 )
+
+        def quantise_w2():
             nc.vector.quantize_mx(
                 out=w2_codes[:].bitcast(FP8X4),
                 scales=w2_scales[:],
@@ -124,7 +134,7 @@ def tile_graphconvlayer_pb_t_kernel(tc, h1, mask, adj, W2, b2, out):
         def row_sums(g):
             deg = work.tile([P, TILES], F32)
             degs[g] = deg
-            if g % SCALAR_SUMS != 0:
+            if g not in SCALAR_SUMS:
                 folded = psum_f.tile([P, TILES, FOLD], F32)
                 for k in range(N // FOLD):
                     nc.tensor.matmul(
@@ -147,12 +157,19 @@ def tile_graphconvlayer_pb_t_kernel(tc, h1, mask, adj, W2, b2, out):
                     out=degs[g][:], in_=folds[g][:], axis=mybir.AxisListType.X, op=ALU.add
                 )
 
+        def gpsimd_copy(out, in_):
+            nc.gpsimd.tensor_scalar(
+                out=out, in0=in_, scalar1=1.0, scalar2=0.0, op0=ALU.mult, op1=ALU.add
+            )
+
         def row_guards(g):
             deg = degs[g]
             safe = work.tile([P, TILES], F32)
-            nc.vector.scalar_tensor_tensor(
-                out=safe[:], in0=deg[:], scalar=0.0, in1=deg[:], op0=ALU.is_equal, op1=ALU.add
+            is_zero = work.tile([P, TILES], F32)
+            nc.gpsimd.tensor_scalar(
+                out=is_zero[:], in0=deg[:], scalar1=0.0, scalar2=1.0, op0=ALU.is_equal, op1=ALU.mult
             )
+            nc.gpsimd.tensor_tensor(out=safe[:], in0=deg[:], in1=is_zero[:], op=ALU.add)
             safes[g] = safe
 
         def row_inverses(g):
@@ -240,7 +257,7 @@ def tile_graphconvlayer_pb_t_kernel(tc, h1, mask, adj, W2, b2, out):
                 if i == 0:
                     spread_mask()
                     spread_bias()
-                scalar_cols = 0 if i % SCALAR_SUMS == 0 else H1_SCALAR_COLS
+                scalar_cols = 0 if i in SCALAR_SUMS else H1_SCALAR_COLS
                 if scalar_cols > 0:
                     regroup_h1(i, nc.scalar.copy, slice(0, scalar_cols))
             if 0 <= i - 1 < B:
@@ -251,8 +268,10 @@ def tile_graphconvlayer_pb_t_kernel(tc, h1, mask, adj, W2, b2, out):
                 adj_mx[i - 2] = quantise(adj_groups[i - 2], "adj", 2, 1)
             if i < B:
                 add_folds(i)
-                regroup_h1(i, nc.vector.tensor_copy, slice(scalar_cols, D))
+                if scalar_cols < D - H1_GPSIMD_COLS:
+                    regroup_h1(i, nc.vector.tensor_copy, slice(scalar_cols, D - H1_GPSIMD_COLS))
                 row_guards(i)
+                regroup_h1(i, gpsimd_copy, slice(D - H1_GPSIMD_COLS, D))
             if 0 <= i - 3 < B:
                 project(i - 3, g_mx[0], g_mx[1])
             if i < B:
@@ -261,5 +280,7 @@ def tile_graphconvlayer_pb_t_kernel(tc, h1, mask, adj, W2, b2, out):
                 aggregate(i - 2)
             if i < B:
                 h1_mx[i] = quantise(h1_groups[i], "h1", 3, 1)
+            if i == W2_ROUND - 1:
+                transpose_w2()
             if i == W2_ROUND:
-                prepare_w2()
+                quantise_w2()

from contextlib import ExitStack

import concourse.mybir as mybir
from concourse.masks import make_identity

F32 = mybir.dt.float32
BF16 = mybir.dt.bfloat16
U32 = mybir.dt.uint32
U8 = mybir.dt.uint8
FP8X4 = mybir.dt.float8_e4m3fn_x4
ALU = mybir.AluOpType
ACT = mybir.ActivationFunctionType

B, N, D = 16, 512, 512
P = 128
PACK = 4
TILES = N // P
HALVES = 2

FLOPS = 2 * B * N * N * D + 2 * B * N * D * D

W2_ROUND = 2
G_PIECES = 2
FOLD = 32
SCALAR_SUMS = (0, 1, 6, 11)
H1_SCALAR_COLS = 384
H1_GPSIMD_COLS = 128
LOADS_AHEAD = 3


def tile_graphconvlayer_pb_t_kernel(tc, h1, mask, adj, W2, b2, out):
    nc = tc.nc
    with ExitStack() as ctx:
        consts = ctx.enter_context(tc.tile_pool(name="consts", bufs=1))
        work = ctx.enter_context(tc.tile_pool(name="work", bufs=2))
        psum_t = ctx.enter_context(tc.psum_pool(name="psum_t", bufs=2))
        psum_f = ctx.enter_context(tc.psum_pool(name="psum_f", bufs=1))
        psum_mx = ctx.enter_context(tc.psum_pool(name="psum_mx", bufs=5))
        ctx.enter_context(tc.manual_schedule())

        adj_rows, h1_rows, degs, safes, inverses = {}, {}, {}, {}, {}
        adj_mx, h1_groups, h1_mx, g_groups, adj_groups = {}, {}, {}, {}, {}
        folds = {}

        def load_adj(g):
            a_rows = work.tile([P, TILES, N], BF16, bufs=LOADS_AHEAD + 2)
            nc.sync.dma_start(out=a_rows[:], in_=adj[g].rearrange("(p t) m -> p t m", t=TILES))
            adj_rows[g] = a_rows

        def load_h1(g):
            h_rows = work.tile([P, PACK, D], BF16, bufs=LOADS_AHEAD + 1)
            nc.sync.dma_start(
                out=h_rows[:].rearrange("p (u e) d -> p u e d", u=HALVES),
                in_=h1[g].rearrange("(u p e) d -> p u e d", u=HALVES, e=2),
            )
            h1_rows[g] = h_rows

        def load_graph(g):
            load_adj(g)
            load_h1(g)

        small_rows = consts.tile([P, D], BF16)
        nc.gpsimd.memset(small_rows[:], 0.0)

        load_adj(0)
        nc.sync.dma_start(out=small_rows[0:B, :], in_=mask)
        nc.sync.dma_start(out=small_rows[B : B + 1, :], in_=b2.unsqueeze(0))
        load_h1(0)
        load_graph(1)
        w2_rows = consts.tile([P, TILES, D], BF16)
        nc.sync.dma_start(out=w2_rows[:], in_=W2.rearrange("(c r) d -> r c d", r=P))
        load_graph(2)

        ident_f32 = consts.tile([P, P], F32)
        make_identity(nc, ident_f32[:])
        ident_bf16 = consts.tile([P, P], BF16)
        make_identity(nc, ident_bf16[:])

        table_warmer = consts.tile([P, 1], F32)
        nc.scalar.activation(out=table_warmer[:], in_=ident_f32[:, 0:1], func=ACT.Gelu)

        mask_cols = consts.tile([P, TILES, B], F32)
        bias_rows = consts.tile([P, D], BF16)

        def spread_mask():
            mask_t = psum_t.tile([P, TILES, P], BF16, tag="transposed")
            for t in range(TILES):
                nc.tensor.transpose(mask_t[:, t, :], small_rows[:, t::TILES], ident_bf16[:])
            nc.scalar.copy(out=mask_cols[:], in_=mask_t[:, :, 0:B])

        def spread_bias():
            bias_all = psum_mx.tile([P, D], F32, tag="mx")
            nc.tensor.matmul(
                bias_all[:], lhsT=ident_bf16[:, B : B + 1].to_broadcast([P, P]), rhs=small_rows[:],
                start=True, stop=True,
            )
            nc.scalar.copy(out=bias_rows[:], in_=bias_all[:])

        w2_group = consts.tile([P, D, PACK], BF16, align_bytes=64)
        w2_codes = consts.tile([P, D], U32, align_bytes=64)
        w2_scales = consts.tile([P, D], U8, align_bytes=64)

        def transpose_w2():
            for c in range(TILES):
                w2_t = psum_t.tile([P, PACK, P], BF16, tag="transposed")
                for j in range(PACK):
                    nc.tensor.transpose(
                        w2_t[:, j, :], w2_rows[:, c, j * P : (j + 1) * P], ident_bf16[:]
                    )
                nc.scalar.copy(
                    out=w2_group[:, c * P : (c + 1) * P, :], in_=w2_t[:].rearrange("p j o -> p o j")
                )

        def quantise_w2():
            nc.vector.quantize_mx(
                out=w2_codes[:].bitcast(FP8X4),
                scales=w2_scales[:],
                in_=w2_group[:].rearrange("p o j -> p (o j)"),
            )

        def quantise(group, operand, depth, pieces):
            codes = work.tile([P, N], U32, align_bytes=64, tag=operand + "_codes", bufs=depth)
            scales = work.tile([P, N], U8, align_bytes=64, tag=operand + "_scales", bufs=depth)
            width = N // pieces
            for k in range(pieces):
                cols = slice(k * width, (k + 1) * width)
                nc.vector.quantize_mx(
                    out=codes[:, cols].bitcast(FP8X4),
                    scales=scales[:, cols],
                    in_=group[:, cols, :].rearrange("p w j -> p (w j)"),
                )
            return codes, scales

        def row_sums(g):
            deg = work.tile([P, TILES], F32)
            degs[g] = deg
            if g not in SCALAR_SUMS:
                folded = psum_f.tile([P, TILES, FOLD], F32)
                for k in range(N // FOLD):
                    nc.tensor.matmul(
                        folded[:], lhsT=ident_bf16[:],
                        rhs=adj_rows[g][:, :, k * FOLD : (k + 1) * FOLD],
                        start=(k == 0), stop=(k == N // FOLD - 1),
                    )
                folds[g] = folded
                return
            unused = work.tile([P, TILES, N], BF16)
            for t in range(TILES):
                nc.scalar.activation(
                    out=unused[:, t, :], in_=adj_rows[g][:, t, :], func=ACT.Copy,
                    accum_out=deg[:, t : t + 1],
                )

        def add_folds(g):
            if g in folds:
                nc.vector.tensor_reduce(
                    out=degs[g][:], in_=folds[g][:], axis=mybir.AxisListType.X, op=ALU.add
                )

        def gpsimd_copy(out, in_):
            nc.gpsimd.tensor_scalar(
                out=out, in0=in_, scalar1=1.0, scalar2=0.0, op0=ALU.mult, op1=ALU.add
            )

        def row_guards(g):
            deg = degs[g]
            safe = work.tile([P, TILES], F32)
            is_zero = work.tile([P, TILES], F32)
            nc.gpsimd.tensor_scalar(
                out=is_zero[:], in0=deg[:], scalar1=0.0, scalar2=1.0, op0=ALU.is_equal, op1=ALU.mult
            )
            nc.gpsimd.tensor_tensor(out=safe[:], in0=deg[:], in1=is_zero[:], op=ALU.add)
            safes[g] = safe

        def row_inverses(g):
            inverse = work.tile([P, TILES], F32)
            nc.vector.reciprocal(out=inverse[:], in_=safes[g][:])
            inverses[g] = inverse

        def normalise_and_transpose(g):
            adj_n = work.tile([P, TILES, N], BF16)
            for t in range(TILES):
                nc.vector.tensor_scalar(
                    out=adj_n[:, t, :], in0=adj_rows[g][:, t, :],
                    scalar1=inverses[g][:, t : t + 1], scalar2=mask_cols[:, t, g : g + 1],
                    op0=ALU.mult, op1=ALU.mult,
                )
            adj_words = adj_n[:].bitcast(F32)
            adj_group = work.tile([P, N, PACK], BF16, align_bytes=64)
            group_words = adj_group[:].bitcast(F32)
            for pair in range(TILES // 2):
                turned = psum_t.tile([P, 2, HALVES, P], F32, tag="transposed")
                for s in range(2):
                    for u in range(HALVES):
                        nc.tensor.transpose(
                            turned[:, s, u, :],
                            adj_words[:, 2 * pair + s, u * P : (u + 1) * P],
                            ident_f32[:],
                        )
                nc.scalar.copy(
                    out=group_words[:, 2 * pair * P : (2 * pair + 2) * P, :].rearrange(
                        "p (s n) u -> p s n u", s=2
                    ),
                    in_=turned[:].rearrange("p s u n -> p s n u"),
                )
            adj_groups[g] = adj_group

        def regroup_h1(g, copy, cols):
            if g not in h1_groups:
                h1_group = work.tile([P, D, PACK], BF16, align_bytes=64)
                h1_groups[g] = h1_group
            copy(
                out=h1_groups[g][:, cols, :].rearrange("p (c i) j -> p c j i", i=4),
                in_=h1_rows[g][:, :, cols].rearrange("p j (c i) -> p c j i", i=4),
            )

        def aggregate(g):
            a_codes, a_scales = adj_mx[g]
            h_codes, h_scales = h1_mx[g]
            g_group = work.tile([P, N, PACK], BF16, align_bytes=64)
            for c in range(TILES):
                nodes = slice(c * P, (c + 1) * P)
                z_t = psum_mx.tile([P, PACK, P], F32, tag="mx")
                for j in range(PACK):
                    feats = slice(j * P, (j + 1) * P)
                    nc.tensor.matmul_mx(
                        out=z_t[:, j, :],
                        lhsT=h_codes[:, feats].bitcast(FP8X4), lhsT_scale=h_scales[:, feats],
                        rhs=a_codes[:, nodes].bitcast(FP8X4), rhs_scale=a_scales[:, nodes],
                        start=True, stop=True,
                    )
                nc.scalar.activation(
                    out=g_group[:, nodes, :], in_=z_t[:].rearrange("p j n -> p n j"), func=ACT.Gelu
                )
            g_groups[g] = g_group

        def project(g, g_codes, g_scales):
            result = work.tile([P, TILES, D], F32, bufs=3)
            out_rows = out[g].rearrange("(p t) o -> p t o", t=TILES)
            for c in range(TILES):
                nodes = slice(c * P, (c + 1) * P)
                acc = psum_mx.tile([P, D], F32, tag="mx")
                nc.tensor.matmul_mx(
                    out=acc[:],
                    lhsT=g_codes[:, nodes].bitcast(FP8X4), lhsT_scale=g_scales[:, nodes],
                    rhs=w2_codes[:].bitcast(FP8X4), rhs_scale=w2_scales[:],
                    start=True, stop=True,
                )
                nc.vector.tensor_tensor(out=result[:, c, :], in0=acc[:], in1=bias_rows[:], op=ALU.add)
                nc.sync.dma_start(out=out_rows[:, c, :], in_=result[:, c, :])

        for i in range(B + 3):
            if i + LOADS_AHEAD < B:
                load_graph(i + LOADS_AHEAD)
            if i < B:
                row_sums(i)
                if i == 0:
                    spread_mask()
                    spread_bias()
                scalar_cols = 0 if i in SCALAR_SUMS else H1_SCALAR_COLS
                if scalar_cols > 0:
                    regroup_h1(i, nc.scalar.copy, slice(0, scalar_cols))
            if 0 <= i - 1 < B:
                normalise_and_transpose(i - 1)
            if 0 <= i - 3 < B:
                g_mx = quantise(g_groups[i - 3], "g", 2, G_PIECES)
            if 0 <= i - 2 < B:
                adj_mx[i - 2] = quantise(adj_groups[i - 2], "adj", 2, 1)
            if i < B:
                add_folds(i)
                if scalar_cols < D - H1_GPSIMD_COLS:
                    regroup_h1(i, nc.vector.tensor_copy, slice(scalar_cols, D - H1_GPSIMD_COLS))
                row_guards(i)
                regroup_h1(i, gpsimd_copy, slice(D - H1_GPSIMD_COLS, D))
            if 0 <= i - 3 < B:
                project(i - 3, g_mx[0], g_mx[1])
            if i < B:
                row_inverses(i)
            if 0 <= i - 2 < B:
                aggregate(i - 2)
            if i < B:
                h1_mx[i] = quantise(h1_groups[i], "h1", 3, 1)
            if i == W2_ROUND - 1:
                transpose_w2()
            if i == W2_ROUND:
                quantise_w2()
